import numpy as np
import ml_dtypes


def mxq(x, axis, fmt="e4m3"):
    dtype, down = {"e4m3": (ml_dtypes.float8_e4m3fn, 7), "e5m2": (ml_dtypes.float8_e5m2, 14)}[fmt]
    v = np.moveaxis(np.asarray(x, np.float32).astype(ml_dtypes.bfloat16).astype(np.float64), axis, -1)
    blocks = v.reshape(v.shape[:-1] + (-1, 32))
    amax = np.abs(blocks).max(-1, keepdims=True)
    byte = np.maximum(np.where(amax > 0, np.frexp(amax)[1] - 1 + 127, 0) - down, 1)
    scale = np.exp2(byte - 127.0)
    codes = (blocks / scale).astype(np.float32).astype(dtype).astype(np.float64)
    return np.moveaxis((codes * scale).reshape(v.shape), -1, axis)


WIDE = False


def mx_kscale(k):
    if not WIDE:
        return np.ones(k)
    levels = np.array([10, -10, 5, -5, 0])
    a = np.random.permutation(np.resize(levels, k // 512 * 4)).reshape(k // 512, 4)
    idx = np.arange(k)
    return np.exp2(a[idx // 512, idx % 128 // 32])


BF16 = ml_dtypes.bfloat16


def bf(x):
    return np.asarray(x, np.float32).astype(BF16)


def f64(x):
    return np.asarray(x).astype(np.float64)


E2M1 = np.array([0.0, 0.5, 1.0, 1.5, 2.0, 3.0, 4.0, 6.0, -0.0, -0.5, -1.0, -1.5, -2.0, -3.0, -4.0, -6.0])


def pack_weight(w, fmt):
    k, n = w.shape
    w = f64(bf(w)).reshape(k // 32, 32, n)
    amax = np.abs(w).max(1)
    if fmt == "e4m3":
        byte = np.frexp(amax)[1] - 1 + 127 - 7
    else:
        mant, ex = np.frexp(amax / 6.0)
        byte = np.where(mant > 0.5, ex, ex - 1) + 127
    byte = np.clip(np.where(amax > 0, byte, 1), 1, 254)
    scaled = (w * np.exp2(127.0 - byte)[:, None, :]).reshape(k, n).astype(np.float32)
    by_word = np.ascontiguousarray(scaled.reshape(k // 512, 128, 4, n).transpose(0, 1, 3, 2))
    if fmt == "e4m3":
        words = by_word.astype(ml_dtypes.float8_e4m3fn).view(np.uint8)
    else:
        c = by_word.astype(ml_dtypes.float4_e2m1fn).view(np.uint8) & 0xF
        words = c[..., 0::2] | (c[..., 1::2] << 4)
    return np.ascontiguousarray(words), np.ascontiguousarray(byte.astype(np.uint8).reshape(k // 512, 16, n))


def unpack_weight(words, scales, fmt):
    g, p, n, _ = words.shape
    if fmt == "e4m3":
        vals = np.ascontiguousarray(words).view(ml_dtypes.float8_e4m3fn).astype(np.float64)
    else:
        nib = np.empty((g, p, n, 4), np.uint8)
        nib[..., 0::2] = words & 0xF
        nib[..., 1::2] = words >> 4
        vals = E2M1[nib]
    vals = vals * np.repeat(np.exp2(scales.astype(np.float64) - 127.0), 8, axis=1)[..., None]
    return vals.transpose(0, 1, 3, 2).reshape(g * 512, n)


N, MI, MO, LMAX = 16, 16384, 256, 3
C = (LMAX + 1) ** 2
FMT = "e4m3"


def setup_inputs():
    s = mx_kscale(MI)
    d = {"x": bf(np.random.standard_normal((N, MI, C)) * s[None, :, None])}
    for l in range(LMAX + 1):
        words, scales = pack_weight(np.random.standard_normal((MI, MO)) / np.sqrt(MI) / s[:, None], FMT)
        d["w%d_words" % l] = words
        d["w%d_scales" % l] = scales
    return d


def reference(x, w0_words, w0_scales, w1_words, w1_scales, w2_words, w2_scales, w3_words, w3_scales):
    xq = mxq(f64(x), 1, "e4m3")
    parts = []
    packed = [(w0_words, w0_scales), (w1_words, w1_scales), (w2_words, w2_scales), (w3_words, w3_scales)]
    for l, (words, scales) in enumerate(packed):
        xl = xq[:, :, l * l:(l + 1) ** 2].transpose(0, 2, 1)
        parts.append((xl @ unpack_weight(words, scales, FMT)).transpose(0, 2, 1))
    return np.concatenate(parts, axis=2)

@@ -1,0 +1,128 @@
+from contextlib import ExitStack
+
+import concourse.mybir as mybir
+from concourse.masks import make_identity
+
+BF16 = mybir.dt.bfloat16
+F32 = mybir.dt.float32
+I32 = mybir.dt.int32
+U32 = mybir.dt.uint32
+U8 = mybir.dt.uint8
+FP8X4 = mybir.dt.float8_e4m3fn_x4
+
+BATCH = 16
+K_TOTAL = 16384
+CHANNELS = 16
+OUTPUTS = 256
+DEGREES = 4
+
+P = 128
+PACK = 4
+K_PASS = P * PACK
+PASSES = K_TOTAL // K_PASS
+PIECES = P // BATCH
+ROUNDS = PASSES // PIECES
+COLUMNS = BATCH * CHANNELS
+PAIRS = CHANNELS // 2
+WINDOW = 128
+O_HALVES = OUTPUTS // P
+QUADRANTS = 4
+SCALE_ROWS = 4
+QUANT_COLUMNS = 4096
+PIECES_PER_QUANT = QUANT_COLUMNS // (COLUMNS * PACK)
+
+FLOPS = 2 * BATCH * CHANNELS * K_TOTAL * OUTPUTS
+
+
+def tile_irrepsstridelinear_k_kernel(
+    tc, x, w0_words, w0_scales, w1_words, w1_scales, w2_words, w2_scales, w3_words, w3_scales, out
+):
+    nc = tc.nc
+    weight_words = [w0_words, w1_words, w2_words, w3_words]
+    weight_scales = [w0_scales, w1_scales, w2_scales, w3_scales]
+
+    with ExitStack() as stack:
+        keep = stack.enter_context(tc.tile_pool(name="keep", bufs=1))
+        x_pool = stack.enter_context(tc.tile_pool(name="x_pool", bufs=ROUNDS))
+        grouped_pool = stack.enter_context(tc.tile_pool(name="grouped_pool", bufs=2))
+        w_pool = stack.enter_context(tc.tile_pool(name="w_pool", bufs=6))
+        bank_pool = stack.enter_context(tc.psum_pool(name="bank_pool", bufs=4))
+        acc_pool = stack.enter_context(tc.psum_pool(name="acc_pool", bufs=2))
+
+        identity = keep.tile([P, P], F32)
+        make_identity(nc, identity[:])
+
+        w_planes = keep.tile([P, DEGREES, PASSES, OUTPUTS], U8, align_bytes=64)
+        for l in range(DEGREES):
+            nc.vector.memset(w_planes[:, l, :, :].bitcast(I32), 0)
+        for l in range(DEGREES):
+            for quadrant in range(QUADRANTS):
+                rows = slice(SCALE_ROWS * quadrant, SCALE_ROWS * (quadrant + 1))
+                nc.sync.dma_start(
+                    out=w_planes[32 * quadrant : 32 * quadrant + SCALE_ROWS, l, :, :].bitcast(I32),
+                    in_=weight_scales[l][:, rows, :].rearrange("g r o -> r g o").bitcast(I32),
+                )
+
+        x_rows = x.rearrange("n (h i) c -> (n h) (i c)", h=PIECES)
+        round_elems = K_PASS * CHANNELS
+        x_raw = []
+        for j in range(ROUNDS):
+            raw = x_pool.tile([P, round_elems], BF16, name="raw")
+            nc.sync.dma_start(out=raw[:], in_=x_rows[:, j * round_elems : (j + 1) * round_elems])
+            x_raw.append(raw)
+
+        x_codes = keep.tile([P, ROUNDS, PIECES, COLUMNS], U32, align_bytes=64)
+        x_planes = keep.tile([P, ROUNDS, PIECES, COLUMNS], U8, align_bytes=64)
+
+        for j in range(ROUNDS):
+            words = x_raw[j][:].bitcast(F32).rearrange("r (p t w) -> r t w p", t=PACK, w=PAIRS)
+            grouped = grouped_pool.tile([P, PIECES, COLUMNS, PACK], BF16, align_bytes=64)
+            for w in range(PAIRS):
+                bank = bank_pool.tile([P, PACK, P], F32)
+                for t in range(PACK):
+                    nc.tensor.transpose(bank[:, t, :], words[:, t, w, :], identity[:])
+                halves = bank[:].bitcast(BF16).rearrange("p t (n h e) -> p e h n t", h=PIECES, e=2)
+                copy = nc.vector.tensor_copy if (j * PAIRS + w) % 3 == 0 else nc.scalar.copy
+                for e in range(2):
+                    c = 2 * w + e
+                    copy(out=grouped[:, :, BATCH * c : BATCH * (c + 1), :], in_=halves[:, e])
+            for first in range(0, PIECES, PIECES_PER_QUANT):
+                pieces = slice(first, first + PIECES_PER_QUANT)
+                nc.vector.quantize_mx(
+                    out=x_codes[:, j, pieces, :].rearrange("p h m -> p (h m)").bitcast(FP8X4),
+                    scales=x_planes[:, j, pieces, :].rearrange("p h m -> p (h m)"),
+                    in_=grouped[:, pieces, :, :].rearrange("p h m t -> p (h m t)"),
+                )
+
+        result = keep.tile([P, BATCH, O_HALVES, CHANNELS], F32)
+        for l in range(DEGREES):
+            first_channel = l * l
+            channels = 2 * l + 1
+            window = (BATCH * first_channel // 64) * 64
+            acc = [acc_pool.tile([P, WINDOW], F32, name="acc%d" % a) for a in range(O_HALVES)]
+            by_round = weight_words[l].rearrange("(h j) p o t -> j p h (o t)", j=ROUNDS)
+            for j in range(ROUNDS):
+                w_codes = w_pool.tile([P, PIECES, OUTPUTS], U32, align_bytes=64)
+                nc.sync.dma_start(out=w_codes[:].bitcast(I32), in_=by_round[j].bitcast(I32))
+                for h in range(PIECES):
+                    g = ROUNDS * h + j
+                    for a in range(O_HALVES):
+                        o_cols = slice(P * a, P * (a + 1))
+                        nc.tensor.matmul_mx(
+                            out=acc[a][:],
+                            lhsT=w_codes[:, h, o_cols].bitcast(FP8X4),
+                            lhsT_scale=w_planes[:, l, g, o_cols],
+                            rhs=x_codes[:, j, h, window : window + WINDOW].bitcast(FP8X4),
+                            rhs_scale=x_planes[:, j, h, window : window + WINDOW],
+                            start=(j == 0 and h == 0),
+                            stop=(j == ROUNDS - 1 and h == PIECES - 1),
+                        )
+            local = BATCH * first_channel - window
+            for a in range(O_HALVES):
+                copy = nc.vector.tensor_copy if a == 0 else nc.scalar.copy
+                copy(
+                    out=result[:, :, a, first_channel : first_channel + channels],
+                    in_=acc[a][:, local : local + BATCH * channels].rearrange("o (c n) -> o n c", n=BATCH),
+                )
+
+        nc.sync.dma_start(out=out.rearrange("n (a o) c -> o n a c", a=O_HALVES), in_=result[:])

@@ -52,6 +52,14 @@ def tile_irrepsstridelinear_k_kernel(
         identity = keep.tile([P, P], F32)
         make_identity(nc, identity[:])
 
+        x_rows = x.rearrange("n (h i) c -> (n h) (i c)", h=PIECES)
+        round_elems = K_PASS * CHANNELS
+        x_raw = []
+        for j in range(ROUNDS):
+            raw = x_pool.tile([P, round_elems], BF16, name="raw")
+            nc.sync.dma_start(out=raw[:], in_=x_rows[:, j * round_elems : (j + 1) * round_elems])
+            x_raw.append(raw)
+
         w_planes = keep.tile([P, DEGREES, PASSES, OUTPUTS], U8, align_bytes=64)
         for l in range(DEGREES):
             nc.vector.memset(w_planes[:, l, :, :].bitcast(I32), 0)
@@ -62,14 +70,6 @@ def tile_irrepsstridelinear_k_kernel(
                     out=w_planes[32 * quadrant : 32 * quadrant + SCALE_ROWS, l, :, :].bitcast(I32),
                     in_=weight_scales[l][:, rows, :].rearrange("g r o -> r g o").bitcast(I32),
                 )
-
-        x_rows = x.rearrange("n (h i) c -> (n h) (i c)", h=PIECES)
-        round_elems = K_PASS * CHANNELS
-        x_raw = []
-        for j in range(ROUNDS):
-            raw = x_pool.tile([P, round_elems], BF16, name="raw")
-            nc.sync.dma_start(out=raw[:], in_=x_rows[:, j * round_elems : (j + 1) * round_elems])
-            x_raw.append(raw)
 
         x_codes = keep.tile([P, ROUNDS, PIECES, COLUMNS], U32, align_bytes=64)
         x_planes = keep.tile([P, ROUNDS, PIECES, COLUMNS], U8, align_bytes=64)

@@ -66,9 +66,9 @@ def tile_irrepsstridelinear_k_kernel(
         for l in range(DEGREES):
             for quadrant in range(QUADRANTS):
                 rows = slice(SCALE_ROWS * quadrant, SCALE_ROWS * (quadrant + 1))
-                nc.sync.dma_start(
-                    out=w_planes[32 * quadrant : 32 * quadrant + SCALE_ROWS, l, :, :].bitcast(I32),
-                    in_=weight_scales[l][:, rows, :].rearrange("g r o -> r g o").bitcast(I32),
+                nc.gpsimd.dma_start(
+                    out=w_planes[32 * quadrant : 32 * quadrant + SCALE_ROWS, l, :, :].bitcast(F32),
+                    in_=weight_scales[l][:, rows, :].rearrange("g r o -> r g o").bitcast(F32),
                 )
 
         x_codes = keep.tile([P, ROUNDS, PIECES, COLUMNS], U32, align_bytes=64)

@@ -31,6 +31,8 @@ SCALE_ROWS = 4
 QUANT_COLUMNS = 4096
 PIECES_PER_QUANT = QUANT_COLUMNS // (COLUMNS * PACK)
 
+assert ROUNDS == QUADRANTS
+
 FLOPS = 2 * BATCH * CHANNELS * K_TOTAL * OUTPUTS
 
 
@@ -52,24 +54,27 @@ def tile_irrepsstridelinear_k_kernel(
         identity = keep.tile([P, P], F32)
         make_identity(nc, identity[:])
 
+        w_planes = keep.tile([P, DEGREES, PASSES, OUTPUTS], U8, align_bytes=64)
+        for l in range(DEGREES):
+            nc.vector.memset(w_planes[:, l, :, :].bitcast(I32), 0)
+
+        def load_scale_rows(l, quadrant):
+            for r in range(SCALE_ROWS):
+                q = SCALE_ROWS * quadrant + r
+                partition = 32 * quadrant + r
+                nc.sync.dma_start(
+                    out=w_planes[partition : partition + 1, l, :, :].bitcast(I32),
+                    in_=weight_scales[l][:, q : q + 1, :].rearrange("g r o -> r g o").bitcast(I32),
+                )
+
         x_rows = x.rearrange("n (h i) c -> (n h) (i c)", h=PIECES)
         round_elems = K_PASS * CHANNELS
         x_raw = []
         for j in range(ROUNDS):
             raw = x_pool.tile([P, round_elems], BF16, name="raw")
             nc.sync.dma_start(out=raw[:], in_=x_rows[:, j * round_elems : (j + 1) * round_elems])
+            load_scale_rows(0, j)
             x_raw.append(raw)
-
-        w_planes = keep.tile([P, DEGREES, PASSES, OUTPUTS], U8, align_bytes=64)
-        for l in range(DEGREES):
-            nc.vector.memset(w_planes[:, l, :, :].bitcast(I32), 0)
-        for l in range(DEGREES):
-            for quadrant in range(QUADRANTS):
-                rows = slice(SCALE_ROWS * quadrant, SCALE_ROWS * (quadrant + 1))
-                nc.gpsimd.dma_start(
-                    out=w_planes[32 * quadrant : 32 * quadrant + SCALE_ROWS, l, :, :].bitcast(F32),
-                    in_=weight_scales[l][:, rows, :].rearrange("g r o -> r g o").bitcast(F32),
-                )
 
         x_codes = keep.tile([P, ROUNDS, PIECES, COLUMNS], U32, align_bytes=64)
         x_planes = keep.tile([P, ROUNDS, PIECES, COLUMNS], U8, align_bytes=64)
@@ -104,6 +109,8 @@ def tile_irrepsstridelinear_k_kernel(
             for j in range(ROUNDS):
                 w_codes = w_pool.tile([P, PIECES, OUTPUTS], U32, align_bytes=64)
                 nc.sync.dma_start(out=w_codes[:].bitcast(I32), in_=by_round[j].bitcast(I32))
+                if l + 1 < DEGREES:
+                    load_scale_rows(l + 1, j)
                 for h in range(PIECES):
                     g = ROUNDS * h + j
                     for a in range(O_HALVES):

@@ -31,8 +31,6 @@ SCALE_ROWS = 4
 QUANT_COLUMNS = 4096
 PIECES_PER_QUANT = QUANT_COLUMNS // (COLUMNS * PACK)
 
-assert ROUNDS == QUADRANTS
-
 FLOPS = 2 * BATCH * CHANNELS * K_TOTAL * OUTPUTS
 
 
@@ -54,27 +52,24 @@ def tile_irrepsstridelinear_k_kernel(
         identity = keep.tile([P, P], F32)
         make_identity(nc, identity[:])
 
-        w_planes = keep.tile([P, DEGREES, PASSES, OUTPUTS], U8, align_bytes=64)
-        for l in range(DEGREES):
-            nc.vector.memset(w_planes[:, l, :, :].bitcast(I32), 0)
-
-        def load_scale_rows(l, quadrant):
-            for r in range(SCALE_ROWS):
-                q = SCALE_ROWS * quadrant + r
-                partition = 32 * quadrant + r
-                nc.sync.dma_start(
-                    out=w_planes[partition : partition + 1, l, :, :].bitcast(I32),
-                    in_=weight_scales[l][:, q : q + 1, :].rearrange("g r o -> r g o").bitcast(I32),
-                )
-
         x_rows = x.rearrange("n (h i) c -> (n h) (i c)", h=PIECES)
         round_elems = K_PASS * CHANNELS
         x_raw = []
         for j in range(ROUNDS):
             raw = x_pool.tile([P, round_elems], BF16, name="raw")
             nc.sync.dma_start(out=raw[:], in_=x_rows[:, j * round_elems : (j + 1) * round_elems])
-            load_scale_rows(0, j)
             x_raw.append(raw)
+
+        w_planes = keep.tile([P, DEGREES, PASSES, OUTPUTS], U8, align_bytes=64)
+        for l in range(DEGREES):
+            nc.vector.memset(w_planes[:, l, :, :].bitcast(I32), 0)
+        for l in range(DEGREES):
+            by_row = weight_scales[l].rearrange("g (quadrant r) o -> r quadrant g o", r=SCALE_ROWS)
+            for r in range(SCALE_ROWS):
+                nc.sync.dma_start(
+                    out=w_planes[r : P : P // QUADRANTS, l, :, :].bitcast(I32),
+                    in_=by_row[r].bitcast(I32),
+                )
 
         x_codes = keep.tile([P, ROUNDS, PIECES, COLUMNS], U32, align_bytes=64)
         x_planes = keep.tile([P, ROUNDS, PIECES, COLUMNS], U8, align_bytes=64)
@@ -109,8 +104,6 @@ def tile_irrepsstridelinear_k_kernel(
             for j in range(ROUNDS):
                 w_codes = w_pool.tile([P, PIECES, OUTPUTS], U32, align_bytes=64)
                 nc.sync.dma_start(out=w_codes[:].bitcast(I32), in_=by_round[j].bitcast(I32))
-                if l + 1 < DEGREES:
-                    load_scale_rows(l + 1, j)
                 for h in range(PIECES):
                     g = ROUNDS * h + j
                     for a in range(O_HALVES):

@@ -31,6 +31,11 @@ SCALE_ROWS = 4
 QUANT_COLUMNS = 4096
 PIECES_PER_QUANT = QUANT_COLUMNS // (COLUMNS * PACK)
 
+ROUND_ELEMS = K_PASS * CHANNELS
+RAW_BYTES = 2 * ROUND_ELEMS
+WEIGHT_LOAD_BYTES = 4 * PIECES * OUTPUTS
+FIRST_LATE_WEIGHT = DEGREES - (ROUNDS * RAW_BYTES) // (ROUNDS * WEIGHT_LOAD_BYTES)
+
 FLOPS = 2 * BATCH * CHANNELS * K_TOTAL * OUTPUTS
 
 
@@ -43,21 +48,40 @@ def tile_irrepsstridelinear_k_kernel(
 
     with ExitStack() as stack:
         keep = stack.enter_context(tc.tile_pool(name="keep", bufs=1))
-        x_pool = stack.enter_context(tc.tile_pool(name="x_pool", bufs=ROUNDS))
+        stream = stack.enter_context(tc.tile_pool(name="stream", bufs=1))
         grouped_pool = stack.enter_context(tc.tile_pool(name="grouped_pool", bufs=2))
-        w_pool = stack.enter_context(tc.tile_pool(name="w_pool", bufs=6))
         bank_pool = stack.enter_context(tc.psum_pool(name="bank_pool", bufs=4))
         acc_pool = stack.enter_context(tc.psum_pool(name="acc_pool", bufs=2))
 
         identity = keep.tile([P, P], F32)
         make_identity(nc, identity[:])
 
+        def load_weight(l):
+            by_round = weight_words[l].rearrange("(h j) p o t -> j p h (o t)", j=ROUNDS)
+            rounds = []
+            for j in range(ROUNDS):
+                codes = stream.tile(
+                    [P, PIECES, OUTPUTS],
+                    U32,
+                    name="w_codes_%d_%d" % (l, j),
+                    align_bytes=64,
+                    offset=WEIGHT_LOAD_BYTES * (ROUNDS * l + j),
+                )
+                nc.sync.dma_start(out=codes[:].bitcast(I32), in_=by_round[j].bitcast(I32))
+                rounds.append(codes)
+            return rounds
+
         x_rows = x.rearrange("n (h i) c -> (n h) (i c)", h=PIECES)
-        round_elems = K_PASS * CHANNELS
         x_raw = []
         for j in range(ROUNDS):
-            raw = x_pool.tile([P, round_elems], BF16, name="raw")
-            nc.sync.dma_start(out=raw[:], in_=x_rows[:, j * round_elems : (j + 1) * round_elems])
+            raw = stream.tile(
+                [P, ROUND_ELEMS],
+                BF16,
+                name="raw_%d" % j,
+                align_bytes=64,
+                offset=WEIGHT_LOAD_BYTES * ROUNDS * FIRST_LATE_WEIGHT + RAW_BYTES * j,
+            )
+            nc.sync.dma_start(out=raw[:], in_=x_rows[:, j * ROUND_ELEMS : (j + 1) * ROUND_ELEMS])
             x_raw.append(raw)
 
         w_planes = keep.tile([P, DEGREES, PASSES, OUTPUTS], U8, align_bytes=64)
@@ -70,6 +94,8 @@ def tile_irrepsstridelinear_k_kernel(
                     out=w_planes[r : P : P // QUADRANTS, l, :, :].bitcast(I32),
                     in_=by_row[r].bitcast(I32),
                 )
+
+        w_codes = [load_weight(l) for l in range(FIRST_LATE_WEIGHT)]
 
         x_codes = keep.tile([P, ROUNDS, PIECES, COLUMNS], U32, align_bytes=64)
         x_planes = keep.tile([P, ROUNDS, PIECES, COLUMNS], U8, align_bytes=64)
@@ -94,23 +120,22 @@ def tile_irrepsstridelinear_k_kernel(
                     in_=grouped[:, pieces, :, :].rearrange("p h m t -> p (h m t)"),
                 )
 
+        w_codes.extend([load_weight(l) for l in range(FIRST_LATE_WEIGHT, DEGREES)])
+
         result = keep.tile([P, BATCH, O_HALVES, CHANNELS], F32)
         for l in range(DEGREES):
             first_channel = l * l
             channels = 2 * l + 1
             window = (BATCH * first_channel // 64) * 64
             acc = [acc_pool.tile([P, WINDOW], F32, name="acc%d" % a) for a in range(O_HALVES)]
-            by_round = weight_words[l].rearrange("(h j) p o t -> j p h (o t)", j=ROUNDS)
             for j in range(ROUNDS):
-                w_codes = w_pool.tile([P, PIECES, OUTPUTS], U32, align_bytes=64)
-                nc.sync.dma_start(out=w_codes[:].bitcast(I32), in_=by_round[j].bitcast(I32))
                 for h in range(PIECES):
                     g = ROUNDS * h + j
                     for a in range(O_HALVES):
                         o_cols = slice(P * a, P * (a + 1))
                         nc.tensor.matmul_mx(
                             out=acc[a][:],
-                            lhsT=w_codes[:, h, o_cols].bitcast(FP8X4),
+                            lhsT=w_codes[l][j][:, h, o_cols].bitcast(FP8X4),
                             lhsT_scale=w_planes[:, l, g, o_cols],
                             rhs=x_codes[:, j, h, window : window + WINDOW].bitcast(FP8X4),
                             rhs_scale=x_planes[:, j, h, window : window + WINDOW],

@@ -31,11 +31,6 @@ SCALE_ROWS = 4
 QUANT_COLUMNS = 4096
 PIECES_PER_QUANT = QUANT_COLUMNS // (COLUMNS * PACK)
 
-ROUND_ELEMS = K_PASS * CHANNELS
-RAW_BYTES = 2 * ROUND_ELEMS
-WEIGHT_LOAD_BYTES = 4 * PIECES * OUTPUTS
-FIRST_LATE_WEIGHT = DEGREES - (ROUNDS * RAW_BYTES) // (ROUNDS * WEIGHT_LOAD_BYTES)
-
 FLOPS = 2 * BATCH * CHANNELS * K_TOTAL * OUTPUTS
 
 
@@ -48,40 +43,21 @@ def tile_irrepsstridelinear_k_kernel(
 
     with ExitStack() as stack:
         keep = stack.enter_context(tc.tile_pool(name="keep", bufs=1))
-        stream = stack.enter_context(tc.tile_pool(name="stream", bufs=1))
+        x_pool = stack.enter_context(tc.tile_pool(name="x_pool", bufs=ROUNDS))
         grouped_pool = stack.enter_context(tc.tile_pool(name="grouped_pool", bufs=2))
+        w_pool = stack.enter_context(tc.tile_pool(name="w_pool", bufs=6))
         bank_pool = stack.enter_context(tc.psum_pool(name="bank_pool", bufs=4))
         acc_pool = stack.enter_context(tc.psum_pool(name="acc_pool", bufs=2))
 
         identity = keep.tile([P, P], F32)
         make_identity(nc, identity[:])
 
-        def load_weight(l):
-            by_round = weight_words[l].rearrange("(h j) p o t -> j p h (o t)", j=ROUNDS)
-            rounds = []
-            for j in range(ROUNDS):
-                codes = stream.tile(
-                    [P, PIECES, OUTPUTS],
-                    U32,
-                    name="w_codes_%d_%d" % (l, j),
-                    align_bytes=64,
-                    offset=WEIGHT_LOAD_BYTES * (ROUNDS * l + j),
-                )
-                nc.sync.dma_start(out=codes[:].bitcast(I32), in_=by_round[j].bitcast(I32))
-                rounds.append(codes)
-            return rounds
-
         x_rows = x.rearrange("n (h i) c -> (n h) (i c)", h=PIECES)
+        round_elems = K_PASS * CHANNELS
         x_raw = []
         for j in range(ROUNDS):
-            raw = stream.tile(
-                [P, ROUND_ELEMS],
-                BF16,
-                name="raw_%d" % j,
-                align_bytes=64,
-                offset=WEIGHT_LOAD_BYTES * ROUNDS * FIRST_LATE_WEIGHT + RAW_BYTES * j,
-            )
-            nc.sync.dma_start(out=raw[:], in_=x_rows[:, j * ROUND_ELEMS : (j + 1) * ROUND_ELEMS])
+            raw = x_pool.tile([P, round_elems], BF16, name="raw")
+            nc.sync.dma_start(out=raw[:], in_=x_rows[:, j * round_elems : (j + 1) * round_elems])
             x_raw.append(raw)
 
         w_planes = keep.tile([P, DEGREES, PASSES, OUTPUTS], U8, align_bytes=64)
@@ -90,12 +66,10 @@ def tile_irrepsstridelinear_k_kernel(
         for l in range(DEGREES):
             by_row = weight_scales[l].rearrange("g (quadrant r) o -> r quadrant g o", r=SCALE_ROWS)
             for r in range(SCALE_ROWS):
-                nc.sync.dma_start(
-                    out=w_planes[r : P : P // QUADRANTS, l, :, :].bitcast(I32),
-                    in_=by_row[r].bitcast(I32),
+                nc.scalar.dma_start(
+                    out=w_planes[r : P : P // QUADRANTS, l, :, :].bitcast(F32),
+                    in_=by_row[r].bitcast(F32),
                 )
-
-        w_codes = [load_weight(l) for l in range(FIRST_LATE_WEIGHT)]
 
         x_codes = keep.tile([P, ROUNDS, PIECES, COLUMNS], U32, align_bytes=64)
         x_planes = keep.tile([P, ROUNDS, PIECES, COLUMNS], U8, align_bytes=64)
@@ -120,22 +94,23 @@ def tile_irrepsstridelinear_k_kernel(
                     in_=grouped[:, pieces, :, :].rearrange("p h m t -> p (h m t)"),
                 )
 
-        w_codes.extend([load_weight(l) for l in range(FIRST_LATE_WEIGHT, DEGREES)])
-
         result = keep.tile([P, BATCH, O_HALVES, CHANNELS], F32)
         for l in range(DEGREES):
             first_channel = l * l
             channels = 2 * l + 1
             window = (BATCH * first_channel // 64) * 64
             acc = [acc_pool.tile([P, WINDOW], F32, name="acc%d" % a) for a in range(O_HALVES)]
+            by_round = weight_words[l].rearrange("(h j) p o t -> j p h (o t)", j=ROUNDS)
             for j in range(ROUNDS):
+                w_codes = w_pool.tile([P, PIECES, OUTPUTS], U32, align_bytes=64)
+                nc.sync.dma_start(out=w_codes[:].bitcast(I32), in_=by_round[j].bitcast(I32))
                 for h in range(PIECES):
                     g = ROUNDS * h + j
                     for a in range(O_HALVES):
                         o_cols = slice(P * a, P * (a + 1))
                         nc.tensor.matmul_mx(
                             out=acc[a][:],
-                            lhsT=w_codes[l][j][:, h, o_cols].bitcast(FP8X4),
+                            lhsT=w_codes[:, h, o_cols].bitcast(FP8X4),
                             lhsT_scale=w_planes[:, l, g, o_cols],
                             rhs=x_codes[:, j, h, window : window + WINDOW].bitcast(FP8X4),
                             rhs_scale=x_planes[:, j, h, window : window + WINDOW],

@@ -31,6 +31,9 @@ SCALE_ROWS = 4
 QUANT_COLUMNS = 4096
 PIECES_PER_QUANT = QUANT_COLUMNS // (COLUMNS * PACK)
 
+LOAD_PIECES = 4
+WEIGHT_BUFFERS = 12
+
 FLOPS = 2 * BATCH * CHANNELS * K_TOTAL * OUTPUTS
 
 
@@ -45,7 +48,7 @@ def tile_irrepsstridelinear_k_kernel(
         keep = stack.enter_context(tc.tile_pool(name="keep", bufs=1))
         x_pool = stack.enter_context(tc.tile_pool(name="x_pool", bufs=ROUNDS))
         grouped_pool = stack.enter_context(tc.tile_pool(name="grouped_pool", bufs=2))
-        w_pool = stack.enter_context(tc.tile_pool(name="w_pool", bufs=6))
+        w_pool = stack.enter_context(tc.tile_pool(name="w_pool", bufs=WEIGHT_BUFFERS))
         bank_pool = stack.enter_context(tc.psum_pool(name="bank_pool", bufs=4))
         acc_pool = stack.enter_context(tc.psum_pool(name="acc_pool", bufs=2))
 
@@ -66,9 +69,9 @@ def tile_irrepsstridelinear_k_kernel(
         for l in range(DEGREES):
             by_row = weight_scales[l].rearrange("g (quadrant r) o -> r quadrant g o", r=SCALE_ROWS)
             for r in range(SCALE_ROWS):
-                nc.scalar.dma_start(
-                    out=w_planes[r : P : P // QUADRANTS, l, :, :].bitcast(F32),
-                    in_=by_row[r].bitcast(F32),
+                nc.sync.dma_start(
+                    out=w_planes[r : P : P // QUADRANTS, l, :, :].bitcast(I32),
+                    in_=by_row[r].bitcast(I32),
                 )
 
         x_codes = keep.tile([P, ROUNDS, PIECES, COLUMNS], U32, align_bytes=64)
@@ -102,21 +105,26 @@ def tile_irrepsstridelinear_k_kernel(
             acc = [acc_pool.tile([P, WINDOW], F32, name="acc%d" % a) for a in range(O_HALVES)]
             by_round = weight_words[l].rearrange("(h j) p o t -> j p h (o t)", j=ROUNDS)
             for j in range(ROUNDS):
-                w_codes = w_pool.tile([P, PIECES, OUTPUTS], U32, align_bytes=64)
-                nc.sync.dma_start(out=w_codes[:].bitcast(I32), in_=by_round[j].bitcast(I32))
-                for h in range(PIECES):
-                    g = ROUNDS * h + j
-                    for a in range(O_HALVES):
-                        o_cols = slice(P * a, P * (a + 1))
-                        nc.tensor.matmul_mx(
-                            out=acc[a][:],
-                            lhsT=w_codes[:, h, o_cols].bitcast(FP8X4),
-                            lhsT_scale=w_planes[:, l, g, o_cols],
-                            rhs=x_codes[:, j, h, window : window + WINDOW].bitcast(FP8X4),
-                            rhs_scale=x_planes[:, j, h, window : window + WINDOW],
-                            start=(j == 0 and h == 0),
-                            stop=(j == ROUNDS - 1 and h == PIECES - 1),
-                        )
+                for first_piece in range(0, PIECES, LOAD_PIECES):
+                    w_codes = w_pool.tile([P, LOAD_PIECES, OUTPUTS], U32, align_bytes=64)
+                    nc.sync.dma_start(
+                        out=w_codes[:].bitcast(I32),
+                        in_=by_round[j][:, first_piece : first_piece + LOAD_PIECES, :].bitcast(I32),
+                    )
+                    for piece in range(LOAD_PIECES):
+                        h = first_piece + piece
+                        g = ROUNDS * h + j
+                        for a in range(O_HALVES):
+                            o_cols = slice(P * a, P * (a + 1))
+                            nc.tensor.matmul_mx(
+                                out=acc[a][:],
+                                lhsT=w_codes[:, piece, o_cols].bitcast(FP8X4),
+                                lhsT_scale=w_planes[:, l, g, o_cols],
+                                rhs=x_codes[:, j, h, window : window + WINDOW].bitcast(FP8X4),
+                                rhs_scale=x_planes[:, j, h, window : window + WINDOW],
+                                start=(j == 0 and h == 0),
+                                stop=(j == ROUNDS - 1 and h == PIECES - 1),
+                            )
             local = BATCH * first_channel - window
             for a in range(O_HALVES):
                 copy = nc.vector.tensor_copy if a == 0 else nc.scalar.copy

@@ -32,7 +32,7 @@ QUANT_COLUMNS = 4096
 PIECES_PER_QUANT = QUANT_COLUMNS // (COLUMNS * PACK)
 
 LOAD_PIECES = 4
-WEIGHT_BUFFERS = 12
+WEIGHT_BUFFERS = 18
 
 FLOPS = 2 * BATCH * CHANNELS * K_TOTAL * OUTPUTS
 
@@ -63,15 +63,14 @@ def tile_irrepsstridelinear_k_kernel(
             nc.sync.dma_start(out=raw[:], in_=x_rows[:, j * round_elems : (j + 1) * round_elems])
             x_raw.append(raw)
 
-        w_planes = keep.tile([P, DEGREES, PASSES, OUTPUTS], U8, align_bytes=64)
-        for l in range(DEGREES):
-            nc.vector.memset(w_planes[:, l, :, :].bitcast(I32), 0)
-        for l in range(DEGREES):
-            by_row = weight_scales[l].rearrange("g (quadrant r) o -> r quadrant g o", r=SCALE_ROWS)
-            for r in range(SCALE_ROWS):
-                nc.sync.dma_start(
-                    out=w_planes[r : P : P // QUADRANTS, l, :, :].bitcast(I32),
-                    in_=by_row[r].bitcast(I32),
+        w_planes = keep.tile([P, PASSES, OUTPUTS], U8, align_bytes=64)
+        nc.vector.memset(w_planes[:].rearrange("p g o -> p (g o)").bitcast(I32), 0)
+        for r in range(SCALE_ROWS):
+            for l in range(DEGREES):
+                by_row = weight_scales[l].rearrange("g (quadrant r) o -> r quadrant g o", r=SCALE_ROWS)
+                nc.gpsimd.dma_start(
+                    out=w_planes[SCALE_ROWS * l + r : P : P // QUADRANTS, :, :].bitcast(F32),
+                    in_=by_row[r].bitcast(F32),
                 )
 
         x_codes = keep.tile([P, ROUNDS, PIECES, COLUMNS], U32, align_bytes=64)
@@ -119,7 +118,7 @@ def tile_irrepsstridelinear_k_kernel(
                             nc.tensor.matmul_mx(
                                 out=acc[a][:],
                                 lhsT=w_codes[:, piece, o_cols].bitcast(FP8X4),
-                                lhsT_scale=w_planes[:, l, g, o_cols],
+                                lhsT_scale=w_planes[SCALE_ROWS * l : P, g, o_cols],
                                 rhs=x_codes[:, j, h, window : window + WINDOW].bitcast(FP8X4),
                                 rhs_scale=x_planes[:, j, h, window : window + WINDOW],
                                 start=(j == 0 and h == 0),

@@ -52,8 +52,21 @@ def tile_irrepsstridelinear_k_kernel(
         bank_pool = stack.enter_context(tc.psum_pool(name="bank_pool", bufs=4))
         acc_pool = stack.enter_context(tc.psum_pool(name="acc_pool", bufs=2))
 
+        stack.enter_context(tc.manual_schedule(engines={mybir.EngineType.SP}))
+
         identity = keep.tile([P, P], F32)
         make_identity(nc, identity[:])
+
+        w_planes = keep.tile([P, PASSES, OUTPUTS], U8, align_bytes=64)
+        nc.vector.memset(w_planes[:].rearrange("p g o -> p (g o)").bitcast(I32), 0)
+        for r in range(SCALE_ROWS):
+            for l in range(DEGREES):
+                by_row = weight_scales[l].rearrange("g (quadrant r) o -> r quadrant g o", r=SCALE_ROWS)
+                rows = w_planes[SCALE_ROWS * l + r : P : P // QUADRANTS, :, :]
+                if l < DEGREES // 2:
+                    nc.sync.dma_start(out=rows.bitcast(I32), in_=by_row[r].bitcast(I32))
+                else:
+                    nc.scalar.dma_start(out=rows.bitcast(F32), in_=by_row[r].bitcast(F32))
 
         x_rows = x.rearrange("n (h i) c -> (n h) (i c)", h=PIECES)
         round_elems = K_PASS * CHANNELS
@@ -62,16 +75,6 @@ def tile_irrepsstridelinear_k_kernel(
             raw = x_pool.tile([P, round_elems], BF16, name="raw")
             nc.sync.dma_start(out=raw[:], in_=x_rows[:, j * round_elems : (j + 1) * round_elems])
             x_raw.append(raw)
-
-        w_planes = keep.tile([P, PASSES, OUTPUTS], U8, align_bytes=64)
-        nc.vector.memset(w_planes[:].rearrange("p g o -> p (g o)").bitcast(I32), 0)
-        for r in range(SCALE_ROWS):
-            for l in range(DEGREES):
-                by_row = weight_scales[l].rearrange("g (quadrant r) o -> r quadrant g o", r=SCALE_ROWS)
-                nc.gpsimd.dma_start(
-                    out=w_planes[SCALE_ROWS * l + r : P : P // QUADRANTS, :, :].bitcast(F32),
-                    in_=by_row[r].bitcast(F32),
-                )
 
         x_codes = keep.tile([P, ROUNDS, PIECES, COLUMNS], U32, align_bytes=64)
         x_planes = keep.tile([P, ROUNDS, PIECES, COLUMNS], U8, align_bytes=64)

@@ -57,6 +57,13 @@ def tile_irrepsstridelinear_k_kernel(
         identity = keep.tile([P, P], F32)
         make_identity(nc, identity[:])
 
+        x_rows = x.rearrange("n (h i) c -> (n h) (i c)", h=PIECES)
+        round_elems = K_PASS * CHANNELS
+        x_raw = [x_pool.tile([P, round_elems], BF16, name="raw") for j in range(ROUNDS)]
+        half_round = round_elems // 2
+        nc.sync.dma_start(out=x_raw[0][:, :half_round], in_=x_rows[:, :half_round])
+        nc.scalar.dma_start(out=x_raw[0][:, half_round:], in_=x_rows[:, half_round:round_elems])
+
         w_planes = keep.tile([P, PASSES, OUTPUTS], U8, align_bytes=64)
         nc.vector.memset(w_planes[:].rearrange("p g o -> p (g o)").bitcast(I32), 0)
         for r in range(SCALE_ROWS):
@@ -68,13 +75,8 @@ def tile_irrepsstridelinear_k_kernel(
                 else:
                     nc.scalar.dma_start(out=rows.bitcast(F32), in_=by_row[r].bitcast(F32))
 
-        x_rows = x.rearrange("n (h i) c -> (n h) (i c)", h=PIECES)
-        round_elems = K_PASS * CHANNELS
-        x_raw = []
-        for j in range(ROUNDS):
-            raw = x_pool.tile([P, round_elems], BF16, name="raw")
-            nc.sync.dma_start(out=raw[:], in_=x_rows[:, j * round_elems : (j + 1) * round_elems])
-            x_raw.append(raw)
+        for j in range(1, ROUNDS):
+            nc.sync.dma_start(out=x_raw[j][:], in_=x_rows[:, j * round_elems : (j + 1) * round_elems])
 
         x_codes = keep.tile([P, ROUNDS, PIECES, COLUMNS], U32, align_bytes=64)
         x_planes = keep.tile([P, ROUNDS, PIECES, COLUMNS], U8, align_bytes=64)
@@ -99,7 +101,7 @@ def tile_irrepsstridelinear_k_kernel(
                     in_=grouped[:, pieces, :, :].rearrange("p h m t -> p (h m t)"),
                 )
 
-        result = keep.tile([P, BATCH, O_HALVES, CHANNELS], F32)
+        result = keep.tile([P, O_HALVES, BATCH, CHANNELS], F32)
         for l in range(DEGREES):
             first_channel = l * l
             channels = 2 * l + 1
@@ -131,8 +133,10 @@ def tile_irrepsstridelinear_k_kernel(
             for a in range(O_HALVES):
                 copy = nc.vector.tensor_copy if a == 0 else nc.scalar.copy
                 copy(
-                    out=result[:, :, a, first_channel : first_channel + channels],
+                    out=result[:, a, :, first_channel : first_channel + channels],
                     in_=acc[a][:, local : local + BATCH * channels].rearrange("o (c n) -> o n c", n=BATCH),
                 )
 
-        nc.sync.dma_start(out=out.rearrange("n (a o) c -> o n a c", a=O_HALVES), in_=result[:])
+        out_halves = out.rearrange("n (a o) c -> a o n c", a=O_HALVES)
+        nc.sync.dma_start(out=out_halves[0], in_=result[:, 0, :, :])
+        nc.scalar.dma_start(out=out_halves[1], in_=result[:, 1, :, :])

@@ -31,8 +31,11 @@ SCALE_ROWS = 4
 QUANT_COLUMNS = 4096
 PIECES_PER_QUANT = QUANT_COLUMNS // (COLUMNS * PACK)
 
-LOAD_PIECES = 4
+LOAD_PASSES = 4
 WEIGHT_BUFFERS = 18
+
+SPLIT_PASSES = 8
+SPLIT_LOAD_PASSES = (8, 4)
 
 FLOPS = 2 * BATCH * CHANNELS * K_TOTAL * OUTPUTS
 
@@ -107,36 +110,58 @@ def tile_irrepsstridelinear_k_kernel(
             channels = 2 * l + 1
             window = (BATCH * first_channel // 64) * 64
             acc = [acc_pool.tile([P, WINDOW], F32, name="acc%d" % a) for a in range(O_HALVES)]
-            by_round = weight_words[l].rearrange("(h j) p o t -> j p h (o t)", j=ROUNDS)
-            for j in range(ROUNDS):
-                for first_piece in range(0, PIECES, LOAD_PIECES):
-                    w_codes = w_pool.tile([P, LOAD_PIECES, OUTPUTS], U32, align_bytes=64)
-                    nc.sync.dma_start(
-                        out=w_codes[:].bitcast(I32),
-                        in_=by_round[j][:, first_piece : first_piece + LOAD_PIECES, :].bitcast(I32),
-                    )
-                    for piece in range(LOAD_PIECES):
-                        h = first_piece + piece
-                        g = ROUNDS * h + j
-                        for a in range(O_HALVES):
-                            o_cols = slice(P * a, P * (a + 1))
-                            nc.tensor.matmul_mx(
-                                out=acc[a][:],
-                                lhsT=w_codes[:, piece, o_cols].bitcast(FP8X4),
-                                lhsT_scale=w_planes[SCALE_ROWS * l : P, g, o_cols],
-                                rhs=x_codes[:, j, h, window : window + WINDOW].bitcast(FP8X4),
-                                rhs_scale=x_planes[:, j, h, window : window + WINDOW],
-                                start=(j == 0 and h == 0),
-                                stop=(j == ROUNDS - 1 and h == PIECES - 1),
-                            )
-            local = BATCH * first_channel - window
-            for a in range(O_HALVES):
+            by_partition = weight_words[l].rearrange("g p o t -> p g (o t)")
+            def load(first_pass, passes, first_half, halves):
+                w_codes = w_pool.tile([P, passes, P * halves], U32, align_bytes=64, name="w_codes")
+                o_bytes = slice(PACK * P * first_half, PACK * P * (first_half + halves))
+                nc.sync.dma_start(
+                    out=w_codes[:].bitcast(I32),
+                    in_=by_partition[:, first_pass : first_pass + passes, o_bytes].bitcast(I32),
+                )
+                return w_codes
+
+            def multiply(g, a, w_codes, place, first_word):
+                h, j = divmod(g, ROUNDS)
+                nc.tensor.matmul_mx(
+                    out=acc[a][:],
+                    lhsT=w_codes[:, place, first_word : first_word + P].bitcast(FP8X4),
+                    lhsT_scale=w_planes[SCALE_ROWS * l : P, g, P * a : P * (a + 1)],
+                    rhs=x_codes[:, j, h, window : window + WINDOW].bitcast(FP8X4),
+                    rhs_scale=x_planes[:, j, h, window : window + WINDOW],
+                    start=(g == 0),
+                    stop=(g == PASSES - 1),
+                )
+
+            def copy_out(a):
+                local = BATCH * first_channel - window
                 copy = nc.vector.tensor_copy if a == 0 else nc.scalar.copy
                 copy(
                     out=result[:, a, :, first_channel : first_channel + channels],
                     in_=acc[a][:, local : local + BATCH * channels].rearrange("o (c n) -> o n c", n=BATCH),
                 )
 
+            last = l == DEGREES - 1
+            for first_pass in range(0, PASSES - SPLIT_PASSES if last else PASSES, LOAD_PASSES):
+                w_codes = load(first_pass, LOAD_PASSES, 0, O_HALVES)
+                for place in range(LOAD_PASSES):
+                    for a in range(O_HALVES):
+                        multiply(first_pass + place, a, w_codes, place, P * a)
+            if not last:
+                for a in range(O_HALVES):
+                    copy_out(a)
+
         out_halves = out.rearrange("n (a o) c -> a o n c", a=O_HALVES)
-        nc.sync.dma_start(out=out_halves[0], in_=result[:, 0, :, :])
-        nc.scalar.dma_start(out=out_halves[1], in_=result[:, 1, :, :])
+        codes = [
+            [
+                (first_pass, passes, load(first_pass, passes, a, 1))
+                for first_pass in range(PASSES - SPLIT_PASSES, PASSES, passes)
+            ]
+            for a, passes in enumerate(SPLIT_LOAD_PASSES)
+        ]
+        for a in range(O_HALVES):
+            for first_pass, passes, w_codes in codes[a]:
+                for place in range(passes):
+                    multiply(first_pass + place, a, w_codes, place, 0)
+            copy_out(a)
+            queue = nc.sync if a == 0 else nc.scalar
+            queue.dma_start(out=out_halves[a], in_=result[:, a, :, :])

@@ -70,7 +70,7 @@ def tile_irrepsstridelinear_k_kernel(
         w_planes = keep.tile([P, PASSES, OUTPUTS], U8, align_bytes=64)
         nc.vector.memset(w_planes[:].rearrange("p g o -> p (g o)").bitcast(I32), 0)
         for r in range(SCALE_ROWS):
-            for l in range(DEGREES):
+            for l in (0, 2, 1, 3):
                 by_row = weight_scales[l].rearrange("g (quadrant r) o -> r quadrant g o", r=SCALE_ROWS)
                 rows = w_planes[SCALE_ROWS * l + r : P : P // QUADRANTS, :, :]
                 if l < DEGREES // 2:
@@ -114,10 +114,12 @@ def tile_irrepsstridelinear_k_kernel(
             def load(first_pass, passes, first_half, halves):
                 w_codes = w_pool.tile([P, passes, P * halves], U32, align_bytes=64, name="w_codes")
                 o_bytes = slice(PACK * P * first_half, PACK * P * (first_half + halves))
-                nc.sync.dma_start(
-                    out=w_codes[:].bitcast(I32),
-                    in_=by_partition[:, first_pass : first_pass + passes, o_bytes].bitcast(I32),
-                )
+                source = by_partition[:, first_pass : first_pass + passes, o_bytes]
+                two_queues = 0 < l < DEGREES - 1 or (l == DEGREES - 1 and first_pass < PASSES // 2)
+                if two_queues and first_pass // passes % 2 == 1:
+                    nc.scalar.dma_start(out=w_codes[:].bitcast(F32), in_=source.bitcast(F32))
+                else:
+                    nc.sync.dma_start(out=w_codes[:].bitcast(I32), in_=source.bitcast(I32))
                 return w_codes
 
             def multiply(g, a, w_codes, place, first_word):

from contextlib import ExitStack

import concourse.mybir as mybir
from concourse.masks import make_identity

BF16 = mybir.dt.bfloat16
F32 = mybir.dt.float32
I32 = mybir.dt.int32
U32 = mybir.dt.uint32
U8 = mybir.dt.uint8
FP8X4 = mybir.dt.float8_e4m3fn_x4

BATCH = 16
K_TOTAL = 16384
CHANNELS = 16
OUTPUTS = 256
DEGREES = 4

P = 128
PACK = 4
K_PASS = P * PACK
PASSES = K_TOTAL // K_PASS
PIECES = P // BATCH
ROUNDS = PASSES // PIECES
COLUMNS = BATCH * CHANNELS
PAIRS = CHANNELS // 2
WINDOW = 128
O_HALVES = OUTPUTS // P
QUADRANTS = 4
SCALE_ROWS = 4
QUANT_COLUMNS = 4096
PIECES_PER_QUANT = QUANT_COLUMNS // (COLUMNS * PACK)

LOAD_PASSES = 4
WEIGHT_BUFFERS = 18

SPLIT_PASSES = 8
SPLIT_LOAD_PASSES = (8, 4)

FLOPS = 2 * BATCH * CHANNELS * K_TOTAL * OUTPUTS


def tile_irrepsstridelinear_k_kernel(
    tc, x, w0_words, w0_scales, w1_words, w1_scales, w2_words, w2_scales, w3_words, w3_scales, out
):
    nc = tc.nc
    weight_words = [w0_words, w1_words, w2_words, w3_words]
    weight_scales = [w0_scales, w1_scales, w2_scales, w3_scales]

    with ExitStack() as stack:
        keep = stack.enter_context(tc.tile_pool(name="keep", bufs=1))
        x_pool = stack.enter_context(tc.tile_pool(name="x_pool", bufs=ROUNDS))
        grouped_pool = stack.enter_context(tc.tile_pool(name="grouped_pool", bufs=2))
        w_pool = stack.enter_context(tc.tile_pool(name="w_pool", bufs=WEIGHT_BUFFERS))
        bank_pool = stack.enter_context(tc.psum_pool(name="bank_pool", bufs=4))
        acc_pool = stack.enter_context(tc.psum_pool(name="acc_pool", bufs=2))

        stack.enter_context(tc.manual_schedule(engines={mybir.EngineType.SP}))

        identity = keep.tile([P, P], F32)
        make_identity(nc, identity[:])

        x_rows = x.rearrange("n (h i) c -> (n h) (i c)", h=PIECES)
        round_elems = K_PASS * CHANNELS
        x_raw = [x_pool.tile([P, round_elems], BF16, name="raw") for j in range(ROUNDS)]
        half_round = round_elems // 2
        nc.sync.dma_start(out=x_raw[0][:, :half_round], in_=x_rows[:, :half_round])
        nc.scalar.dma_start(out=x_raw[0][:, half_round:], in_=x_rows[:, half_round:round_elems])

        w_planes = keep.tile([P, PASSES, OUTPUTS], U8, align_bytes=64)
        nc.vector.memset(w_planes[:].rearrange("p g o -> p (g o)").bitcast(I32), 0)
        for r in range(SCALE_ROWS):
            for l in (0, 2, 1, 3):
                by_row = weight_scales[l].rearrange("g (quadrant r) o -> r quadrant g o", r=SCALE_ROWS)
                rows = w_planes[SCALE_ROWS * l + r : P : P // QUADRANTS, :, :]
                if l < DEGREES // 2:
                    nc.sync.dma_start(out=rows.bitcast(I32), in_=by_row[r].bitcast(I32))
                else:
                    nc.scalar.dma_start(out=rows.bitcast(F32), in_=by_row[r].bitcast(F32))

        for j in range(1, ROUNDS):
            nc.sync.dma_start(out=x_raw[j][:], in_=x_rows[:, j * round_elems : (j + 1) * round_elems])

        x_codes = keep.tile([P, ROUNDS, PIECES, COLUMNS], U32, align_bytes=64)
        x_planes = keep.tile([P, ROUNDS, PIECES, COLUMNS], U8, align_bytes=64)

        for j in range(ROUNDS):
            words = x_raw[j][:].bitcast(F32).rearrange("r (p t w) -> r t w p", t=PACK, w=PAIRS)
            grouped = grouped_pool.tile([P, PIECES, COLUMNS, PACK], BF16, align_bytes=64)
            for w in range(PAIRS):
                bank = bank_pool.tile([P, PACK, P], F32)
                for t in range(PACK):
                    nc.tensor.transpose(bank[:, t, :], words[:, t, w, :], identity[:])
                halves = bank[:].bitcast(BF16).rearrange("p t (n h e) -> p e h n t", h=PIECES, e=2)
                copy = nc.vector.tensor_copy if (j * PAIRS + w) % 3 == 0 else nc.scalar.copy
                for e in range(2):
                    c = 2 * w + e
                    copy(out=grouped[:, :, BATCH * c : BATCH * (c + 1), :], in_=halves[:, e])
            for first in range(0, PIECES, PIECES_PER_QUANT):
                pieces = slice(first, first + PIECES_PER_QUANT)
                nc.vector.quantize_mx(
                    out=x_codes[:, j, pieces, :].rearrange("p h m -> p (h m)").bitcast(FP8X4),
                    scales=x_planes[:, j, pieces, :].rearrange("p h m -> p (h m)"),
                    in_=grouped[:, pieces, :, :].rearrange("p h m t -> p (h m t)"),
                )

        result = keep.tile([P, O_HALVES, BATCH, CHANNELS], F32)
        for l in range(DEGREES):
            first_channel = l * l
            channels = 2 * l + 1
            window = (BATCH * first_channel // 64) * 64
            acc = [acc_pool.tile([P, WINDOW], F32, name="acc%d" % a) for a in range(O_HALVES)]
            by_partition = weight_words[l].rearrange("g p o t -> p g (o t)")
            def load(first_pass, passes, first_half, halves):
                w_codes = w_pool.tile([P, passes, P * halves], U32, align_bytes=64, name="w_codes")
                o_bytes = slice(PACK * P * first_half, PACK * P * (first_half + halves))
                source = by_partition[:, first_pass : first_pass + passes, o_bytes]
                two_queues = 0 < l < DEGREES - 1 or (l == DEGREES - 1 and first_pass < PASSES // 2)
                if two_queues and first_pass // passes % 2 == 1:
                    nc.scalar.dma_start(out=w_codes[:].bitcast(F32), in_=source.bitcast(F32))
                else:
                    nc.sync.dma_start(out=w_codes[:].bitcast(I32), in_=source.bitcast(I32))
                return w_codes

            def multiply(g, a, w_codes, place, first_word):
                h, j = divmod(g, ROUNDS)
                nc.tensor.matmul_mx(
                    out=acc[a][:],
                    lhsT=w_codes[:, place, first_word : first_word + P].bitcast(FP8X4),
                    lhsT_scale=w_planes[SCALE_ROWS * l : P, g, P * a : P * (a + 1)],
                    rhs=x_codes[:, j, h, window : window + WINDOW].bitcast(FP8X4),
                    rhs_scale=x_planes[:, j, h, window : window + WINDOW],
                    start=(g == 0),
                    stop=(g == PASSES - 1),
                )

            def copy_out(a):
                local = BATCH * first_channel - window
                copy = nc.vector.tensor_copy if a == 0 else nc.scalar.copy
                copy(
                    out=result[:, a, :, first_channel : first_channel + channels],
                    in_=acc[a][:, local : local + BATCH * channels].rearrange("o (c n) -> o n c", n=BATCH),
                )

            last = l == DEGREES - 1
            for first_pass in range(0, PASSES - SPLIT_PASSES if last else PASSES, LOAD_PASSES):
                w_codes = load(first_pass, LOAD_PASSES, 0, O_HALVES)
                for place in range(LOAD_PASSES):
                    for a in range(O_HALVES):
                        multiply(first_pass + place, a, w_codes, place, P * a)
            if not last:
                for a in range(O_HALVES):
                    copy_out(a)

        out_halves = out.rearrange("n (a o) c -> a o n c", a=O_HALVES)
        codes = [
            [
                (first_pass, passes, load(first_pass, passes, a, 1))
                for first_pass in range(PASSES - SPLIT_PASSES, PASSES, passes)
            ]
            for a, passes in enumerate(SPLIT_LOAD_PASSES)
        ]
        for a in range(O_HALVES):
            for first_pass, passes, w_codes in codes[a]:
                for place in range(passes):
                    multiply(first_pass + place, a, w_codes, place, 0)
            copy_out(a)
            queue = nc.sync if a == 0 else nc.scalar
            queue.dma_start(out=out_halves[a], in_=result[:, a, :, :])
